import numpy as np
import ml_dtypes


def mxq(x, axis, fmt="e4m3"):
    dtype, down = {"e4m3": (ml_dtypes.float8_e4m3fn, 7), "e5m2": (ml_dtypes.float8_e5m2, 14)}[fmt]
    v = np.moveaxis(np.asarray(x, np.float32).astype(ml_dtypes.bfloat16).astype(np.float64), axis, -1)
    blocks = v.reshape(v.shape[:-1] + (-1, 32))
    amax = np.abs(blocks).max(-1, keepdims=True)
    byte = np.maximum(np.where(amax > 0, np.frexp(amax)[1] - 1 + 127, 0) - down, 1)
    scale = np.exp2(byte - 127.0)
    codes = (blocks / scale).astype(np.float32).astype(dtype).astype(np.float64)
    return np.moveaxis((codes * scale).reshape(v.shape), -1, axis)


WIDE = False


def mx_kscale(k):
    if not WIDE:
        return np.ones(k)
    levels = np.array([10, -10, 5, -5, 0])
    if k % 512:
        return np.exp2(np.random.permutation(np.resize(levels, k // 32))).repeat(32)
    a = np.empty((k // 512, 16))
    for p in range(k // 512):
        a[p, :8] = np.random.permutation(np.resize(levels, 8))
        for g in range(8):
            far = levels[np.abs(levels - a[p, g]) >= 10]
            a[p, g + 8] = far[np.random.randint(len(far))]
    return np.exp2(a.ravel()).repeat(32)


BF16 = ml_dtypes.bfloat16


def bf(x):
    return np.asarray(x, np.float32).astype(BF16)


def f64(x):
    return np.asarray(x).astype(np.float64)


BATCH, IN_Q, OUT_Q = 8192, 256, 128
K, N = 4 * IN_Q, 4 * OUT_Q


def _quat_block_matrix(W):
    Ww, Wx, Wy, Wz = W[..., 0], W[..., 1], W[..., 2], W[..., 3]
    row_w = np.stack([Ww, -Wx, -Wy, -Wz], axis=0)
    row_x = np.stack([Wx, Ww, -Wz, Wy], axis=0)
    row_y = np.stack([Wy, Wz, Ww, -Wx], axis=0)
    row_z = np.stack([Wz, -Wy, Wx, Ww], axis=0)
    return np.stack([row_w, row_x, row_y, row_z], axis=0)


def setup_inputs():
    s = mx_kscale(K)[::4]
    sigma = 1.0 / np.sqrt(2.0 * (IN_Q + OUT_Q))
    return {"x": bf(np.random.standard_normal((BATCH, IN_Q, 4)) * s[None, :, None]),
            "W": bf(np.random.standard_normal((OUT_Q, IN_Q, 4)) * sigma / s[None, :, None]),
            "B": bf(np.random.standard_normal((OUT_Q, 4)) * 0.2)}


def reference(x, W, B):
    Wq = mxq(f64(W).reshape(OUT_Q, K), 1, "e4m3").reshape(OUT_Q, IN_Q, 4)
    M = _quat_block_matrix(Wq)
    Mk = M.transpose(3, 1, 2, 0).reshape(K, N)
    xk = f64(x).reshape(BATCH, K)
    s = (mxq(xk, 1, "e4m3") @ Mk).reshape(BATCH, OUT_Q, 4)
    s = s + f64(B)
    return np.tanh(s)

@@ -1,0 +1,264 @@
+from contextlib import ExitStack
+
+import concourse.mybir as mybir
+from concourse.masks import make_identity
+
+F32 = mybir.dt.float32
+BF16 = mybir.dt.bfloat16
+U32 = mybir.dt.uint32
+U8 = mybir.dt.uint8
+FP8X4 = mybir.dt.float8_e4m3fn_x4
+ACT = mybir.ActivationFunctionType
+ALU = mybir.AluOpType
+
+P = 128
+BATCH, IN_Q, OUT_Q = 8192, 256, 128
+K, N = 4 * IN_Q, 4 * OUT_Q
+FLOPS = 2 * BATCH * K * N
+ROW_TILES = BATCH // P
+R = 2
+GROUPS = ROW_TILES // R
+STORE_GROUPS = 2
+HEAD_CHUNKS = [1, 1, 2, 4, 4, 4]
+MAIN_CHUNK = 8
+MAIN_BUFS = 4
+LAG_MX = 3
+LAG_ADD = 4
+LAG_TANH = 5
+OUT_TILES = STORE_GROUPS * R
+SYNC_FROM = 48
+FINE_FROM = 52
+SPLIT_FROM = 56
+WARM_FIRST = 5
+
+PLACE = [
+    (0, 0, 1, 1, 0, 1.0),
+    (0, 1, 3, 1, 1, -1.0),
+    (1, 1, 2, 2, 0, 1.0),
+    (1, 0, 1, 1, 1, 1.0),
+    (1, 2, 1, 1, 3, -1.0),
+    (2, 0, 2, 1, 2, 1.0),
+    (2, 2, 1, 1, 0, 1.0),
+    (2, 3, 1, 1, 1, -1.0),
+    (3, 0, 1, 1, 3, 1.0),
+    (3, 1, 1, 1, 2, -1.0),
+    (3, 2, 1, 1, 1, 1.0),
+    (3, 3, 1, 1, 0, 1.0),
+]
+
+
+def vector_copies(j, r):
+    return r == R - 1 and j % 8 in (1, 4, 6)
+
+
+def tile_quatnetpytorchdenselayer_t_kernel(tc, x, W, B, out):
+    nc = tc.nc
+    xv = x.rearrange("(p t) i c -> p t (i c)", t=ROW_TILES)
+    ov = out.rearrange("(p t) o d -> p t (o d)", t=ROW_TILES)
+
+    with ExitStack() as ctx:
+        const = ctx.enter_context(tc.tile_pool(name="const", bufs=1))
+        xhead = ctx.enter_context(tc.tile_pool(name="xhead", bufs=1))
+        xmain = ctx.enter_context(tc.tile_pool(name="xmain", bufs=MAIN_BUFS))
+        gpool = ctx.enter_context(tc.tile_pool(name="gpool", bufs=4))
+        cpool = ctx.enter_context(tc.tile_pool(name="cpool", bufs=LAG_MX + 3))
+        opool = ctx.enter_context(tc.tile_pool(name="opool", bufs=8))
+        ps_t = ctx.enter_context(tc.psum_pool(name="ps_t", bufs=4))
+        ps_o = ctx.enter_context(tc.psum_pool(name="ps_o", bufs=4))
+        ctx.enter_context(tc.manual_schedule())
+
+        ones = const.tile([P, P], BF16, name="ones")
+        nc.vector.memset(ones[:], 1.0)
+        zeros = const.tile([P, N], BF16, name="zeros")
+        nc.vector.memset(zeros[:], 0.0)
+        warm = const.tile([P, 1], F32, name="warm")
+        nc.vector.memset(warm[:], 0.0)
+        b_row = const.tile([P, N], BF16, name="b_row")
+        nc.vector.memset(b_row[:], 0.0)
+        nc.scalar.activation(out=warm[:], in_=warm[:], func=ACT.Tanh)
+        ident = const.tile([P, P], F32, name="ident")
+        make_identity(nc, ident[:])
+
+        w_sb = const.tile([P, IN_Q, 4], BF16, name="w_sb")
+        nc.sync.dma_start(out=w_sb[:], in_=W)
+
+        chunks = []
+        t0 = 0
+        for n_rows in HEAD_CHUNKS:
+            chunks.append((t0, n_rows))
+            t0 += n_rows
+        while t0 < ROW_TILES:
+            chunks.append((t0, MAIN_CHUNK))
+            t0 += MAIN_CHUNK
+        where = {}
+
+        def load_chunk(ci):
+            first, n_rows = chunks[ci]
+            if ci < len(HEAD_CHUNKS):
+                xs = xhead.tile([P, n_rows, K], BF16, name="xh%d" % ci)
+            else:
+                xs = xmain.tile([P, MAIN_CHUNK, K], BF16, name="xs", tag="xs")
+            nc.sync.dma_start(out=xs[:], in_=xv[:, first : first + n_rows, :])
+            words = xs[:].bitcast(F32)
+            for r in range(n_rows):
+                where[first + r] = (words, r)
+
+        n_first = len(HEAD_CHUNKS) + MAIN_BUFS
+        for ci in range(min(n_first, len(chunks))):
+            load_chunk(ci)
+            if ci == 2:
+                nc.sync.dma_start(out=b_row[0:1, :], in_=B.rearrange("(a o) d -> a (o d)", a=1))
+        last_of_chunk = {}
+        for ci in range(len(HEAD_CHUNKS), len(chunks)):
+            last_of_chunk[chunks[ci][0] + chunks[ci][1] - 1] = ci
+
+        banks = {}
+        grouped = {}
+        codes = {}
+        planes = {}
+        accs = {}
+        outs = {}
+
+        def keep_clock(bank, times):
+            for i_warm in range(times):
+                nc.tensor.matmul(out=bank[:].rearrange("p q b -> p (q b)"), lhsT=ones[:], rhs=zeros[:], start=True, stop=True)
+
+        def transposes(j, warmers=0):
+            for r in range(R):
+                words, idx = where[j * R + r]
+                xt = ps_t.tile([P, 4, P], F32, name="xt", tag="xt")
+                if r == 0:
+                    keep_clock(xt, warmers)
+                for q in range(4):
+                    nc.tensor.transpose(xt[:, q, :], words[:, idx, 256 * (q // 2) + q % 2 : 256 * (q // 2 + 1) : 2], ident[:])
+                banks[(j, r)] = xt
+                ci = last_of_chunk.get(j * R + r)
+                if ci is not None and ci + MAIN_BUFS < len(chunks):
+                    load_chunk(ci + MAIN_BUFS)
+
+        def copies(j):
+            grp = gpool.tile([P, R * K], BF16, name="grp", tag="grp", align_bytes=64)
+            grouped[j] = grp
+            gw = grp[:].bitcast(F32).rearrange("p (r g b u) -> p r g b u", r=R, g=2, u=2)
+            for r in range(R):
+                src = banks[(j, r)][:].rearrange("p (g u) b -> p g b u", u=2)
+                if vector_copies(j, r):
+                    nc.vector.tensor_copy(out=gw[:, r], in_=src)
+                else:
+                    nc.scalar.copy(out=gw[:, r], in_=src)
+
+        def quantise(j):
+            cw = cpool.tile([P, R * 2 * P], U32, name="cw", tag="cw", align_bytes=64)
+            sc = cpool.tile([P, R * 2 * P], U8, name="sc", tag="sc", align_bytes=64)
+            nc.vector.quantize_mx(out=cw[:].bitcast(FP8X4), scales=sc[:], in_=grouped[j][:])
+            codes[j] = cw
+            planes[j] = sc
+
+        def passes(j):
+            for r in range(R):
+                acc = ps_o.tile([P, N], F32, name="acc", tag="acc")
+                for g in range(2):
+                    col = (2 * r + g) * P
+                    nc.tensor.matmul_mx(
+                        out=acc[:],
+                        lhsT=codes[j][:, col : col + P].bitcast(FP8X4),
+                        lhsT_scale=planes[j][:, col : col + P],
+                        rhs=mk_codes[:, g * N : (g + 1) * N].bitcast(FP8X4),
+                        rhs_scale=mk_planes[:, g * N : (g + 1) * N],
+                        start=(g == 0),
+                        stop=(g == 1),
+                    )
+                accs[(j, r)] = acc
+
+        def adds(j):
+            big, half = divmod(j, STORE_GROUPS)
+            if half == 0:
+                outs[big] = opool.tile([P, STORE_GROUPS * R, N], F32, name="ot", tag="ot")
+            for r in range(R):
+                nc.vector.tensor_tensor(out=outs[big][:, half * R + r, :], in0=accs[(j, r)][:], in1=bias[:], op=ALU.add)
+
+        def finish(j):
+            first = j * R
+            big, pos = divmod(first, OUT_TILES)
+            pieces = [(first + r, 1) for r in range(R)] if first >= SPLIT_FROM else [(first, R)]
+            for t, n_rows in pieces:
+                part = outs[big][:, t - big * OUT_TILES : t - big * OUT_TILES + n_rows, :]
+                nc.scalar.activation(out=part, in_=part, func=ACT.Tanh)
+                if t >= FINE_FROM:
+                    nc.sync.dma_start(out=ov[:, t : t + n_rows, :], in_=part)
+            if first < FINE_FROM and pos + R == OUT_TILES:
+                queue = nc.sync if first >= SYNC_FROM else nc.gpsimd
+                queue.dma_start(out=ov[:, big * OUT_TILES : (big + 1) * OUT_TILES, :], in_=outs[big][:])
+
+        mk_t = const.tile([P, 4, K], BF16, name="mk_t")
+        mk_v = mk_t[:].rearrange("p d (i c) -> p d i c", c=4)
+        for d, c_out, n_c, step, c_in, sign in PLACE:
+            dst = mk_v[:, d, :, c_out : c_out + (n_c - 1) * step + 1 : step]
+            src = w_sb[:, :, c_in : c_in + (n_c - 1) * step + 1 : step]
+            if d < 2:
+                nc.vector.tensor_scalar(out=dst, in0=src, scalar1=sign, scalar2=None, op0=ALU.mult)
+            elif d == 2:
+                nc.scalar.mul(out=dst, in_=src, mul=sign)
+            else:
+                nc.gpsimd.tensor_scalar(out=dst, in0=src, scalar1=sign, scalar2=0.0, op0=ALU.mult, op1=ALU.add)
+
+        transposes(0, WARM_FIRST)
+        copies(0)
+        transposes(1, 1)
+        copies(1)
+
+        pb = ps_o.tile([P, N], F32, name="acc", tag="acc")
+        nc.tensor.matmul(out=pb[:], lhsT=ones[:], rhs=b_row[:], start=True, stop=True)
+        bias = const.tile([P, N], F32, name="bias")
+
+        mk_w = mk_t[:].bitcast(F32)
+        mk_g = const.tile([P, 2, 4 * N], BF16, name="mk_g", align_bytes=64)
+        mk_gw = mk_g[:].bitcast(F32).rearrange("p g (o d u) -> p g o d u", d=4, u=2)
+        mk_codes = const.tile([P, 2 * N], U32, name="mk_codes", align_bytes=64)
+        mk_planes = const.tile([P, 2 * N], U8, name="mk_planes", align_bytes=64)
+        mk_banks = {}
+        for dh in range(2):
+            for g in range(2):
+                if (g, dh) == (1, 1):
+                    nc.vector.tensor_copy(out=bias[:], in_=pb[:])
+                pm = ps_o.tile([P, 4, P], F32, name="acc", tag="acc")
+                if (g, dh) == (0, 1):
+                    keep_clock(pm, 1)
+                for dl in range(2):
+                    for u in range(2):
+                        nc.tensor.transpose(pm[:, 2 * dl + u, :], mk_w[:, 2 * dh + dl, 256 * g + u : 256 * (g + 1) : 2], ident[:])
+                mk_banks[(g, dh)] = pm
+
+        def mk_exit(g, dh):
+            dst = mk_gw[:, g, :, 2 * dh : 2 * dh + 2, :]
+            src = mk_banks[(g, dh)][:].rearrange("p (l u) o -> p o l u", u=2)
+            if g == 0:
+                nc.vector.tensor_copy(out=dst, in_=src)
+            else:
+                nc.scalar.copy(out=dst, in_=src)
+
+        mk_exit(0, 0)
+        mk_exit(1, 0)
+        quantise(0)
+        mk_exit(0, 1)
+        mk_exit(1, 1)
+        for g in range(2):
+            nc.vector.quantize_mx(
+                out=mk_codes[:, g * N : (g + 1) * N].bitcast(FP8X4),
+                scales=mk_planes[:, g * N : (g + 1) * N],
+                in_=mk_g[:, g, :],
+            )
+
+        for s in range(2, GROUPS + LAG_TANH):
+            if s < GROUPS:
+                transposes(s, 1 if s <= LAG_MX else 0)
+            if 0 <= s - LAG_MX < GROUPS:
+                passes(s - LAG_MX)
+            if 0 <= s - LAG_ADD < GROUPS:
+                adds(s - LAG_ADD)
+            if 0 <= s - LAG_TANH < GROUPS:
+                finish(s - LAG_TANH)
+            if s < GROUPS:
+                copies(s)
+            if s - 1 < GROUPS:
+                quantise(s - 1)

@@ -26,10 +26,11 @@ LAG_MX = 3
 LAG_ADD = 4
 LAG_TANH = 5
 OUT_TILES = STORE_GROUPS * R
-SYNC_FROM = 48
 FINE_FROM = 52
 SPLIT_FROM = 56
 WARM_FIRST = 5
+SORT_FROM = 3
+SORT_AHEAD = 2
 
 PLACE = [
     (0, 0, 1, 1, 0, 1.0),
@@ -60,6 +61,7 @@ def tile_quatnetpytorchdenselayer_t_kernel(tc, x, W, B, out):
         const = ctx.enter_context(tc.tile_pool(name="const", bufs=1))
         xhead = ctx.enter_context(tc.tile_pool(name="xhead", bufs=1))
         xmain = ctx.enter_context(tc.tile_pool(name="xmain", bufs=MAIN_BUFS))
+        spool = ctx.enter_context(tc.tile_pool(name="spool", bufs=SORT_AHEAD + 2))
         gpool = ctx.enter_context(tc.tile_pool(name="gpool", bufs=4))
         cpool = ctx.enter_context(tc.tile_pool(name="cpool", bufs=LAG_MX + 3))
         opool = ctx.enter_context(tc.tile_pool(name="opool", bufs=8))
@@ -91,6 +93,8 @@ def tile_quatnetpytorchdenselayer_t_kernel(tc, x, W, B, out):
             chunks.append((t0, MAIN_CHUNK))
             t0 += MAIN_CHUNK
         where = {}
+        plain = {}
+        in_order = {}
 
         def load_chunk(ci):
             first, n_rows = chunks[ci]
@@ -102,6 +106,7 @@ def tile_quatnetpytorchdenselayer_t_kernel(tc, x, W, B, out):
             words = xs[:].bitcast(F32)
             for r in range(n_rows):
                 where[first + r] = (words, r)
+                plain[first + r] = (xs, r)
 
         n_first = len(HEAD_CHUNKS) + MAIN_BUFS
         for ci in range(min(n_first, len(chunks))):
@@ -123,6 +128,20 @@ def tile_quatnetpytorchdenselayer_t_kernel(tc, x, W, B, out):
             for i_warm in range(times):
                 nc.tensor.matmul(out=bank[:].rearrange("p q b -> p (q b)"), lhsT=ones[:], rhs=zeros[:], start=True, stop=True)
 
+        def sort_words(j):
+            t = j * R + R - 1
+            xs, idx = plain[t]
+            st = spool.tile([P, K], BF16, name="st", tag="st")
+            nc.gpsimd.tensor_scalar(
+                out=st[:].rearrange("b (u w e) -> b u w e", u=2, e=2),
+                in0=xs[:, idx, :].rearrange("b (w u e) -> b u w e", u=2, e=2),
+                scalar1=1.0,
+                scalar2=0.0,
+                op0=ALU.mult,
+                op1=ALU.add,
+            )
+            in_order[t] = st[:].bitcast(F32)
+
         def transposes(j, warmers=0):
             for r in range(R):
                 words, idx = where[j * R + r]
@@ -130,7 +149,11 @@ def tile_quatnetpytorchdenselayer_t_kernel(tc, x, W, B, out):
                 if r == 0:
                     keep_clock(xt, warmers)
                 for q in range(4):
-                    nc.tensor.transpose(xt[:, q, :], words[:, idx, 256 * (q // 2) + q % 2 : 256 * (q // 2 + 1) : 2], ident[:])
+                    if j * R + r in in_order:
+                        col = 256 * (q % 2) + P * (q // 2)
+                        nc.tensor.transpose(xt[:, q, :], in_order[j * R + r][:, col : col + P], ident[:])
+                    else:
+                        nc.tensor.transpose(xt[:, q, :], words[:, idx, 256 * (q // 2) + q % 2 : 256 * (q // 2 + 1) : 2], ident[:])
                 banks[(j, r)] = xt
                 ci = last_of_chunk.get(j * R + r)
                 if ci is not None and ci + MAIN_BUFS < len(chunks):
@@ -187,8 +210,7 @@ def tile_quatnetpytorchdenselayer_t_kernel(tc, x, W, B, out):
                 if t >= FINE_FROM:
                     nc.sync.dma_start(out=ov[:, t : t + n_rows, :], in_=part)
             if first < FINE_FROM and pos + R == OUT_TILES:
-                queue = nc.sync if first >= SYNC_FROM else nc.gpsimd
-                queue.dma_start(out=ov[:, big * OUT_TILES : (big + 1) * OUT_TILES, :], in_=outs[big][:])
+                nc.sync.dma_start(out=ov[:, big * OUT_TILES : (big + 1) * OUT_TILES, :], in_=outs[big][:])
 
         mk_t = const.tile([P, 4, K], BF16, name="mk_t")
         mk_v = mk_t[:].rearrange("p d (i c) -> p d i c", c=4)
@@ -249,9 +271,13 @@ def tile_quatnetpytorchdenselayer_t_kernel(tc, x, W, B, out):
                 in_=mk_g[:, g, :],
             )
 
+        for j in range(SORT_FROM, SORT_FROM + SORT_AHEAD):
+            sort_words(j)
         for s in range(2, GROUPS + LAG_TANH):
             if s < GROUPS:
                 transposes(s, 1 if s <= LAG_MX else 0)
+            if SORT_FROM <= s and s + SORT_AHEAD < GROUPS:
+                sort_words(s + SORT_AHEAD)
             if 0 <= s - LAG_MX < GROUPS:
                 passes(s - LAG_MX)
             if 0 <= s - LAG_ADD < GROUPS:

@@ -131,14 +131,10 @@ def tile_quatnetpytorchdenselayer_t_kernel(tc, x, W, B, out):
         def sort_words(j):
             t = j * R + R - 1
             xs, idx = plain[t]
-            st = spool.tile([P, K], BF16, name="st", tag="st")
-            nc.gpsimd.tensor_scalar(
-                out=st[:].rearrange("b (u w e) -> b u w e", u=2, e=2),
-                in0=xs[:, idx, :].rearrange("b (w u e) -> b u w e", u=2, e=2),
-                scalar1=1.0,
-                scalar2=0.0,
-                op0=ALU.mult,
-                op1=ALU.add,
+            st = spool.tile([P, K // 2], U32, name="st", tag="st")
+            nc.gpsimd.tensor_copy(
+                out=st[:].rearrange("b (u w) -> b u w", u=2),
+                in_=xs[:, idx, :].bitcast(U32).rearrange("b (w u) -> b u w", u=2),
             )
             in_order[t] = st[:].bitcast(F32)
 
@@ -272,11 +268,12 @@ def tile_quatnetpytorchdenselayer_t_kernel(tc, x, W, B, out):
             )
 
         for j in range(SORT_FROM, SORT_FROM + SORT_AHEAD):
-            sort_words(j)
+            if j % 4 != 0:
+                sort_words(j)
         for s in range(2, GROUPS + LAG_TANH):
             if s < GROUPS:
                 transposes(s, 1 if s <= LAG_MX else 0)
-            if SORT_FROM <= s and s + SORT_AHEAD < GROUPS:
+            if SORT_FROM <= s and s + SORT_AHEAD < GROUPS and (s + SORT_AHEAD) % 4 != 0:
                 sort_words(s + SORT_AHEAD)
             if 0 <= s - LAG_MX < GROUPS:
                 passes(s - LAG_MX)

@@ -28,24 +28,11 @@ LAG_TANH = 5
 OUT_TILES = STORE_GROUPS * R
 FINE_FROM = 52
 SPLIT_FROM = 56
-WARM_FIRST = 5
+WARM_FIRST = 3
 SORT_FROM = 3
 SORT_AHEAD = 2
 
-PLACE = [
-    (0, 0, 1, 1, 0, 1.0),
-    (0, 1, 3, 1, 1, -1.0),
-    (1, 1, 2, 2, 0, 1.0),
-    (1, 0, 1, 1, 1, 1.0),
-    (1, 2, 1, 1, 3, -1.0),
-    (2, 0, 2, 1, 2, 1.0),
-    (2, 2, 1, 1, 0, 1.0),
-    (2, 3, 1, 1, 1, -1.0),
-    (3, 0, 1, 1, 3, 1.0),
-    (3, 1, 1, 1, 2, -1.0),
-    (3, 2, 1, 1, 1, 1.0),
-    (3, 3, 1, 1, 0, 1.0),
-]
+SIGN = [[1, -1, -1, -1], [1, 1, -1, 1], [1, 1, 1, -1], [1, -1, 1, 1]]
 
 
 def vector_copies(j, r):
@@ -63,7 +50,7 @@ def tile_quatnetpytorchdenselayer_t_kernel(tc, x, W, B, out):
         xmain = ctx.enter_context(tc.tile_pool(name="xmain", bufs=MAIN_BUFS))
         spool = ctx.enter_context(tc.tile_pool(name="spool", bufs=SORT_AHEAD + 2))
         gpool = ctx.enter_context(tc.tile_pool(name="gpool", bufs=4))
-        cpool = ctx.enter_context(tc.tile_pool(name="cpool", bufs=LAG_MX + 3))
+        cpool = ctx.enter_context(tc.tile_pool(name="cpool", bufs=6))
         opool = ctx.enter_context(tc.tile_pool(name="opool", bufs=8))
         ps_t = ctx.enter_context(tc.psum_pool(name="ps_t", bufs=4))
         ps_o = ctx.enter_context(tc.psum_pool(name="ps_o", bufs=4))
@@ -80,6 +67,10 @@ def tile_quatnetpytorchdenselayer_t_kernel(tc, x, W, B, out):
         nc.scalar.activation(out=warm[:], in_=warm[:], func=ACT.Tanh)
         ident = const.tile([P, P], F32, name="ident")
         make_identity(nc, ident[:])
+        signed = {}
+        for sign in (1, -1):
+            signed[sign] = const.tile([P, P], BF16, name="ident_p" if sign == 1 else "ident_m")
+            nc.vector.tensor_scalar(out=signed[sign][:], in0=ident[:], scalar1=float(sign), scalar2=None, op0=ALU.mult)
 
         w_sb = const.tile([P, IN_Q, 4], BF16, name="w_sb")
         nc.sync.dma_start(out=w_sb[:], in_=W)
@@ -126,7 +117,7 @@ def tile_quatnetpytorchdenselayer_t_kernel(tc, x, W, B, out):
 
         def keep_clock(bank, times):
             for i_warm in range(times):
-                nc.tensor.matmul(out=bank[:].rearrange("p q b -> p (q b)"), lhsT=ones[:], rhs=zeros[:], start=True, stop=True)
+                nc.tensor.matmul(out=bank[:], lhsT=ones[:], rhs=zeros[:], start=True, stop=True)
 
         def sort_words(j):
             t = j * R + R - 1
@@ -138,12 +129,10 @@ def tile_quatnetpytorchdenselayer_t_kernel(tc, x, W, B, out):
             )
             in_order[t] = st[:].bitcast(F32)
 
-        def transposes(j, warmers=0):
+        def transposes(j):
             for r in range(R):
                 words, idx = where[j * R + r]
                 xt = ps_t.tile([P, 4, P], F32, name="xt", tag="xt")
-                if r == 0:
-                    keep_clock(xt, warmers)
                 for q in range(4):
                     if j * R + r in in_order:
                         col = 256 * (q % 2) + P * (q // 2)
@@ -208,71 +197,67 @@ def tile_quatnetpytorchdenselayer_t_kernel(tc, x, W, B, out):
             if first < FINE_FROM and pos + R == OUT_TILES:
                 nc.sync.dma_start(out=ov[:, big * OUT_TILES : (big + 1) * OUT_TILES, :], in_=outs[big][:])
 
-        mk_t = const.tile([P, 4, K], BF16, name="mk_t")
-        mk_v = mk_t[:].rearrange("p d (i c) -> p d i c", c=4)
-        for d, c_out, n_c, step, c_in, sign in PLACE:
-            dst = mk_v[:, d, :, c_out : c_out + (n_c - 1) * step + 1 : step]
-            src = w_sb[:, :, c_in : c_in + (n_c - 1) * step + 1 : step]
-            if d < 2:
-                nc.vector.tensor_scalar(out=dst, in0=src, scalar1=sign, scalar2=None, op0=ALU.mult)
-            elif d == 2:
-                nc.scalar.mul(out=dst, in_=src, mul=sign)
-            else:
-                nc.gpsimd.tensor_scalar(out=dst, in0=src, scalar1=sign, scalar2=0.0, op0=ALU.mult, op1=ALU.add)
-
-        transposes(0, WARM_FIRST)
-        copies(0)
-        transposes(1, 1)
-        copies(1)
-
-        pb = ps_o.tile([P, N], F32, name="acc", tag="acc")
-        nc.tensor.matmul(out=pb[:], lhsT=ones[:], rhs=b_row[:], start=True, stop=True)
-        bias = const.tile([P, N], F32, name="bias")
-
-        mk_w = mk_t[:].bitcast(F32)
         mk_g = const.tile([P, 2, 4 * N], BF16, name="mk_g", align_bytes=64)
-        mk_gw = mk_g[:].bitcast(F32).rearrange("p g (o d u) -> p g o d u", d=4, u=2)
         mk_codes = const.tile([P, 2 * N], U32, name="mk_codes", align_bytes=64)
         mk_planes = const.tile([P, 2 * N], U8, name="mk_planes", align_bytes=64)
+        bias = const.tile([P, N], F32, name="bias")
         mk_banks = {}
-        for dh in range(2):
-            for g in range(2):
-                if (g, dh) == (1, 1):
-                    nc.vector.tensor_copy(out=bias[:], in_=pb[:])
-                pm = ps_o.tile([P, 4, P], F32, name="acc", tag="acc")
-                if (g, dh) == (0, 1):
-                    keep_clock(pm, 1)
+
+        def mk_signed(g):
+            for dh in range(2):
+                pm = ps_o.tile([P, 2, 4, P], BF16, name="acc", tag="acc")
                 for dl in range(2):
-                    for u in range(2):
-                        nc.tensor.transpose(pm[:, 2 * dl + u, :], mk_w[:, 2 * dh + dl, 256 * g + u : 256 * (g + 1) : 2], ident[:])
+                    d = 2 * dh + dl
+                    for c in range(4):
+                        nc.tensor.matmul(
+                            out=pm[:, dl, c, :],
+                            lhsT=w_sb[:, P * g : P * (g + 1), c ^ d],
+                            rhs=signed[SIGN[d][c]][:],
+                            start=True,
+                            stop=True,
+                        )
                 mk_banks[(g, dh)] = pm
 
         def mk_exit(g, dh):
-            dst = mk_gw[:, g, :, 2 * dh : 2 * dh + 2, :]
-            src = mk_banks[(g, dh)][:].rearrange("p (l u) o -> p o l u", u=2)
-            if g == 0:
+            dst = mk_g[:, g, :].rearrange("p (o h q) -> p o h q", h=2, q=8)[:, :, dh, :]
+            src = mk_banks[(g, dh)][:].rearrange("p l c o -> p o (l c)")
+            if dh == 0:
                 nc.vector.tensor_copy(out=dst, in_=src)
             else:
                 nc.scalar.copy(out=dst, in_=src)
 
-        mk_exit(0, 0)
-        mk_exit(1, 0)
-        quantise(0)
-        mk_exit(0, 1)
-        mk_exit(1, 1)
-        for g in range(2):
+        def mk_quantise(g):
             nc.vector.quantize_mx(
                 out=mk_codes[:, g * N : (g + 1) * N].bitcast(FP8X4),
                 scales=mk_planes[:, g * N : (g + 1) * N],
                 in_=mk_g[:, g, :],
             )
 
+        first = ps_o.tile([P, N], F32, name="acc", tag="acc")
+        keep_clock(first, WARM_FIRST)
+        mk_signed(0)
+        mk_exit(0, 0)
+        mk_exit(0, 1)
+        mk_signed(1)
+        mk_exit(1, 0)
+        mk_exit(1, 1)
+        transposes(0)
+        copies(0)
+        mk_quantise(0)
+        mk_quantise(1)
+        quantise(0)
+        transposes(1)
+        copies(1)
+        pb = ps_o.tile([P, N], F32, name="acc", tag="acc")
+        nc.tensor.matmul(out=pb[:], lhsT=ones[:], rhs=b_row[:], start=True, stop=True)
+        nc.vector.tensor_copy(out=bias[:], in_=pb[:])
+
         for j in range(SORT_FROM, SORT_FROM + SORT_AHEAD):
             if j % 4 != 0:
                 sort_words(j)
         for s in range(2, GROUPS + LAG_TANH):
             if s < GROUPS:
-                transposes(s, 1 if s <= LAG_MX else 0)
+                transposes(s)
             if SORT_FROM <= s and s + SORT_AHEAD < GROUPS and (s + SORT_AHEAD) % 4 != 0:
                 sort_words(s + SORT_AHEAD)
             if 0 <= s - LAG_MX < GROUPS:

@@ -19,7 +19,7 @@ ROW_TILES = BATCH // P
 R = 2
 GROUPS = ROW_TILES // R
 STORE_GROUPS = 2
-HEAD_CHUNKS = [1, 1, 2, 4, 4, 4]
+HEAD_CHUNKS = [1, 1, 2, 2, 2, 4, 4]
 MAIN_CHUNK = 8
 MAIN_BUFS = 4
 LAG_MX = 3
@@ -28,7 +28,7 @@ LAG_TANH = 5
 OUT_TILES = STORE_GROUPS * R
 FINE_FROM = 52
 SPLIT_FROM = 56
-WARM_FIRST = 3
+WARM_FIRST = 4
 SORT_FROM = 3
 SORT_AHEAD = 2
 
@@ -56,10 +56,10 @@ def tile_quatnetpytorchdenselayer_t_kernel(tc, x, W, B, out):
         ps_o = ctx.enter_context(tc.psum_pool(name="ps_o", bufs=4))
         ctx.enter_context(tc.manual_schedule())
 
+        zeros = const.tile([P, N], BF16, name="zeros")
+        nc.vector.memset(zeros[:].bitcast(U32), 0)
         ones = const.tile([P, P], BF16, name="ones")
         nc.vector.memset(ones[:], 1.0)
-        zeros = const.tile([P, N], BF16, name="zeros")
-        nc.vector.memset(zeros[:], 0.0)
         warm = const.tile([P, 1], F32, name="warm")
         nc.vector.memset(warm[:], 0.0)
         b_row = const.tile([P, N], BF16, name="b_row")
@@ -117,7 +117,7 @@ def tile_quatnetpytorchdenselayer_t_kernel(tc, x, W, B, out):
 
         def keep_clock(bank, times):
             for i_warm in range(times):
-                nc.tensor.matmul(out=bank[:], lhsT=ones[:], rhs=zeros[:], start=True, stop=True)
+                nc.tensor.matmul(out=bank[:], lhsT=zeros[:, :P], rhs=zeros[:], start=True, stop=True)
 
         def sort_words(j):
             t = j * R + R - 1

@@ -16,6 +16,7 @@ BATCH, IN_Q, OUT_Q = 8192, 256, 128
 K, N = 4 * IN_Q, 4 * OUT_Q
 FLOPS = 2 * BATCH * K * N
 ROW_TILES = BATCH // P
+BLOCK_TILES = 8
 R = 2
 GROUPS = ROW_TILES // R
 STORE_GROUPS = 2
@@ -41,8 +42,8 @@ def vector_copies(j, r):
 
 def tile_quatnetpytorchdenselayer_t_kernel(tc, x, W, B, out):
     nc = tc.nc
-    xv = x.rearrange("(p t) i c -> p t (i c)", t=ROW_TILES)
-    ov = out.rearrange("(p t) o d -> p t (o d)", t=ROW_TILES)
+    xv = x.rearrange("(b p r) i c -> p b r (i c)", p=P, r=BLOCK_TILES)
+    ov = out.rearrange("(b p r) o d -> p b r (o d)", p=P, r=BLOCK_TILES)
 
     with ExitStack() as ctx:
         const = ctx.enter_context(tc.tile_pool(name="const", bufs=1))
@@ -93,7 +94,7 @@ def tile_quatnetpytorchdenselayer_t_kernel(tc, x, W, B, out):
                 xs = xhead.tile([P, n_rows, K], BF16, name="xh%d" % ci)
             else:
                 xs = xmain.tile([P, MAIN_CHUNK, K], BF16, name="xs", tag="xs")
-            nc.sync.dma_start(out=xs[:], in_=xv[:, first : first + n_rows, :])
+            nc.sync.dma_start(out=xs[:], in_=xv[:, first // BLOCK_TILES, first % BLOCK_TILES : first % BLOCK_TILES + n_rows, :])
             words = xs[:].bitcast(F32)
             for r in range(n_rows):
                 where[first + r] = (words, r)
@@ -193,9 +194,10 @@ def tile_quatnetpytorchdenselayer_t_kernel(tc, x, W, B, out):
                 part = outs[big][:, t - big * OUT_TILES : t - big * OUT_TILES + n_rows, :]
                 nc.scalar.activation(out=part, in_=part, func=ACT.Tanh)
                 if t >= FINE_FROM:
-                    nc.sync.dma_start(out=ov[:, t : t + n_rows, :], in_=part)
+                    nc.sync.dma_start(out=ov[:, t // BLOCK_TILES, t % BLOCK_TILES : t % BLOCK_TILES + n_rows, :], in_=part)
             if first < FINE_FROM and pos + R == OUT_TILES:
-                nc.sync.dma_start(out=ov[:, big * OUT_TILES : (big + 1) * OUT_TILES, :], in_=outs[big][:])
+                pos_block = big * OUT_TILES % BLOCK_TILES
+                nc.sync.dma_start(out=ov[:, t // BLOCK_TILES, pos_block : pos_block + OUT_TILES, :], in_=outs[big][:])
 
         mk_g = const.tile([P, 2, 4 * N], BF16, name="mk_g", align_bytes=64)
         mk_codes = const.tile([P, 2 * N], U32, name="mk_codes", align_bytes=64)

from contextlib import ExitStack

import concourse.mybir as mybir
from concourse.masks import make_identity

F32 = mybir.dt.float32
BF16 = mybir.dt.bfloat16
U32 = mybir.dt.uint32
U8 = mybir.dt.uint8
FP8X4 = mybir.dt.float8_e4m3fn_x4
ACT = mybir.ActivationFunctionType
ALU = mybir.AluOpType

P = 128
BATCH, IN_Q, OUT_Q = 8192, 256, 128
K, N = 4 * IN_Q, 4 * OUT_Q
FLOPS = 2 * BATCH * K * N
ROW_TILES = BATCH // P
BLOCK_TILES = 8
R = 2
GROUPS = ROW_TILES // R
STORE_GROUPS = 2
HEAD_CHUNKS = [1, 1, 2, 2, 2, 4, 4]
MAIN_CHUNK = 8
MAIN_BUFS = 4
LAG_MX = 3
LAG_ADD = 4
LAG_TANH = 5
OUT_TILES = STORE_GROUPS * R
FINE_FROM = 52
SPLIT_FROM = 56
WARM_FIRST = 4
SORT_FROM = 3
SORT_AHEAD = 2

SIGN = [[1, -1, -1, -1], [1, 1, -1, 1], [1, 1, 1, -1], [1, -1, 1, 1]]


def vector_copies(j, r):
    return r == R - 1 and j % 8 in (1, 4, 6)


def tile_quatnetpytorchdenselayer_t_kernel(tc, x, W, B, out):
    nc = tc.nc
    xv = x.rearrange("(b p r) i c -> p b r (i c)", p=P, r=BLOCK_TILES)
    ov = out.rearrange("(b p r) o d -> p b r (o d)", p=P, r=BLOCK_TILES)

    with ExitStack() as ctx:
        const = ctx.enter_context(tc.tile_pool(name="const", bufs=1))
        xhead = ctx.enter_context(tc.tile_pool(name="xhead", bufs=1))
        xmain = ctx.enter_context(tc.tile_pool(name="xmain", bufs=MAIN_BUFS))
        spool = ctx.enter_context(tc.tile_pool(name="spool", bufs=SORT_AHEAD + 2))
        gpool = ctx.enter_context(tc.tile_pool(name="gpool", bufs=4))
        cpool = ctx.enter_context(tc.tile_pool(name="cpool", bufs=6))
        opool = ctx.enter_context(tc.tile_pool(name="opool", bufs=8))
        ps_t = ctx.enter_context(tc.psum_pool(name="ps_t", bufs=4))
        ps_o = ctx.enter_context(tc.psum_pool(name="ps_o", bufs=4))
        ctx.enter_context(tc.manual_schedule())

        zeros = const.tile([P, N], BF16, name="zeros")
        nc.vector.memset(zeros[:].bitcast(U32), 0)
        ones = const.tile([P, P], BF16, name="ones")
        nc.vector.memset(ones[:], 1.0)
        warm = const.tile([P, 1], F32, name="warm")
        nc.vector.memset(warm[:], 0.0)
        b_row = const.tile([P, N], BF16, name="b_row")
        nc.vector.memset(b_row[:], 0.0)
        nc.scalar.activation(out=warm[:], in_=warm[:], func=ACT.Tanh)
        ident = const.tile([P, P], F32, name="ident")
        make_identity(nc, ident[:])
        signed = {}
        for sign in (1, -1):
            signed[sign] = const.tile([P, P], BF16, name="ident_p" if sign == 1 else "ident_m")
            nc.vector.tensor_scalar(out=signed[sign][:], in0=ident[:], scalar1=float(sign), scalar2=None, op0=ALU.mult)

        w_sb = const.tile([P, IN_Q, 4], BF16, name="w_sb")
        nc.sync.dma_start(out=w_sb[:], in_=W)

        chunks = []
        t0 = 0
        for n_rows in HEAD_CHUNKS:
            chunks.append((t0, n_rows))
            t0 += n_rows
        while t0 < ROW_TILES:
            chunks.append((t0, MAIN_CHUNK))
            t0 += MAIN_CHUNK
        where = {}
        plain = {}
        in_order = {}

        def load_chunk(ci):
            first, n_rows = chunks[ci]
            if ci < len(HEAD_CHUNKS):
                xs = xhead.tile([P, n_rows, K], BF16, name="xh%d" % ci)
            else:
                xs = xmain.tile([P, MAIN_CHUNK, K], BF16, name="xs", tag="xs")
            nc.sync.dma_start(out=xs[:], in_=xv[:, first // BLOCK_TILES, first % BLOCK_TILES : first % BLOCK_TILES + n_rows, :])
            words = xs[:].bitcast(F32)
            for r in range(n_rows):
                where[first + r] = (words, r)
                plain[first + r] = (xs, r)

        n_first = len(HEAD_CHUNKS) + MAIN_BUFS
        for ci in range(min(n_first, len(chunks))):
            load_chunk(ci)
            if ci == 2:
                nc.sync.dma_start(out=b_row[0:1, :], in_=B.rearrange("(a o) d -> a (o d)", a=1))
        last_of_chunk = {}
        for ci in range(len(HEAD_CHUNKS), len(chunks)):
            last_of_chunk[chunks[ci][0] + chunks[ci][1] - 1] = ci

        banks = {}
        grouped = {}
        codes = {}
        planes = {}
        accs = {}
        outs = {}

        def keep_clock(bank, times):
            for i_warm in range(times):
                nc.tensor.matmul(out=bank[:], lhsT=zeros[:, :P], rhs=zeros[:], start=True, stop=True)

        def sort_words(j):
            t = j * R + R - 1
            xs, idx = plain[t]
            st = spool.tile([P, K // 2], U32, name="st", tag="st")
            nc.gpsimd.tensor_copy(
                out=st[:].rearrange("b (u w) -> b u w", u=2),
                in_=xs[:, idx, :].bitcast(U32).rearrange("b (w u) -> b u w", u=2),
            )
            in_order[t] = st[:].bitcast(F32)

        def transposes(j):
            for r in range(R):
                words, idx = where[j * R + r]
                xt = ps_t.tile([P, 4, P], F32, name="xt", tag="xt")
                for q in range(4):
                    if j * R + r in in_order:
                        col = 256 * (q % 2) + P * (q // 2)
                        nc.tensor.transpose(xt[:, q, :], in_order[j * R + r][:, col : col + P], ident[:])
                    else:
                        nc.tensor.transpose(xt[:, q, :], words[:, idx, 256 * (q // 2) + q % 2 : 256 * (q // 2 + 1) : 2], ident[:])
                banks[(j, r)] = xt
                ci = last_of_chunk.get(j * R + r)
                if ci is not None and ci + MAIN_BUFS < len(chunks):
                    load_chunk(ci + MAIN_BUFS)

        def copies(j):
            grp = gpool.tile([P, R * K], BF16, name="grp", tag="grp", align_bytes=64)
            grouped[j] = grp
            gw = grp[:].bitcast(F32).rearrange("p (r g b u) -> p r g b u", r=R, g=2, u=2)
            for r in range(R):
                src = banks[(j, r)][:].rearrange("p (g u) b -> p g b u", u=2)
                if vector_copies(j, r):
                    nc.vector.tensor_copy(out=gw[:, r], in_=src)
                else:
                    nc.scalar.copy(out=gw[:, r], in_=src)

        def quantise(j):
            cw = cpool.tile([P, R * 2 * P], U32, name="cw", tag="cw", align_bytes=64)
            sc = cpool.tile([P, R * 2 * P], U8, name="sc", tag="sc", align_bytes=64)
            nc.vector.quantize_mx(out=cw[:].bitcast(FP8X4), scales=sc[:], in_=grouped[j][:])
            codes[j] = cw
            planes[j] = sc

        def passes(j):
            for r in range(R):
                acc = ps_o.tile([P, N], F32, name="acc", tag="acc")
                for g in range(2):
                    col = (2 * r + g) * P
                    nc.tensor.matmul_mx(
                        out=acc[:],
                        lhsT=codes[j][:, col : col + P].bitcast(FP8X4),
                        lhsT_scale=planes[j][:, col : col + P],
                        rhs=mk_codes[:, g * N : (g + 1) * N].bitcast(FP8X4),
                        rhs_scale=mk_planes[:, g * N : (g + 1) * N],
                        start=(g == 0),
                        stop=(g == 1),
                    )
                accs[(j, r)] = acc

        def adds(j):
            big, half = divmod(j, STORE_GROUPS)
            if half == 0:
                outs[big] = opool.tile([P, STORE_GROUPS * R, N], F32, name="ot", tag="ot")
            for r in range(R):
                nc.vector.tensor_tensor(out=outs[big][:, half * R + r, :], in0=accs[(j, r)][:], in1=bias[:], op=ALU.add)

        def finish(j):
            first = j * R
            big, pos = divmod(first, OUT_TILES)
            pieces = [(first + r, 1) for r in range(R)] if first >= SPLIT_FROM else [(first, R)]
            for t, n_rows in pieces:
                part = outs[big][:, t - big * OUT_TILES : t - big * OUT_TILES + n_rows, :]
                nc.scalar.activation(out=part, in_=part, func=ACT.Tanh)
                if t >= FINE_FROM:
                    nc.sync.dma_start(out=ov[:, t // BLOCK_TILES, t % BLOCK_TILES : t % BLOCK_TILES + n_rows, :], in_=part)
            if first < FINE_FROM and pos + R == OUT_TILES:
                pos_block = big * OUT_TILES % BLOCK_TILES
                nc.sync.dma_start(out=ov[:, t // BLOCK_TILES, pos_block : pos_block + OUT_TILES, :], in_=outs[big][:])

        mk_g = const.tile([P, 2, 4 * N], BF16, name="mk_g", align_bytes=64)
        mk_codes = const.tile([P, 2 * N], U32, name="mk_codes", align_bytes=64)
        mk_planes = const.tile([P, 2 * N], U8, name="mk_planes", align_bytes=64)
        bias = const.tile([P, N], F32, name="bias")
        mk_banks = {}

        def mk_signed(g):
            for dh in range(2):
                pm = ps_o.tile([P, 2, 4, P], BF16, name="acc", tag="acc")
                for dl in range(2):
                    d = 2 * dh + dl
                    for c in range(4):
                        nc.tensor.matmul(
                            out=pm[:, dl, c, :],
                            lhsT=w_sb[:, P * g : P * (g + 1), c ^ d],
                            rhs=signed[SIGN[d][c]][:],
                            start=True,
                            stop=True,
                        )
                mk_banks[(g, dh)] = pm

        def mk_exit(g, dh):
            dst = mk_g[:, g, :].rearrange("p (o h q) -> p o h q", h=2, q=8)[:, :, dh, :]
            src = mk_banks[(g, dh)][:].rearrange("p l c o -> p o (l c)")
            if dh == 0:
                nc.vector.tensor_copy(out=dst, in_=src)
            else:
                nc.scalar.copy(out=dst, in_=src)

        def mk_quantise(g):
            nc.vector.quantize_mx(
                out=mk_codes[:, g * N : (g + 1) * N].bitcast(FP8X4),
                scales=mk_planes[:, g * N : (g + 1) * N],
                in_=mk_g[:, g, :],
            )

        first = ps_o.tile([P, N], F32, name="acc", tag="acc")
        keep_clock(first, WARM_FIRST)
        mk_signed(0)
        mk_exit(0, 0)
        mk_exit(0, 1)
        mk_signed(1)
        mk_exit(1, 0)
        mk_exit(1, 1)
        transposes(0)
        copies(0)
        mk_quantise(0)
        mk_quantise(1)
        quantise(0)
        transposes(1)
        copies(1)
        pb = ps_o.tile([P, N], F32, name="acc", tag="acc")
        nc.tensor.matmul(out=pb[:], lhsT=ones[:], rhs=b_row[:], start=True, stop=True)
        nc.vector.tensor_copy(out=bias[:], in_=pb[:])

        for j in range(SORT_FROM, SORT_FROM + SORT_AHEAD):
            if j % 4 != 0:
                sort_words(j)
        for s in range(2, GROUPS + LAG_TANH):
            if s < GROUPS:
                transposes(s)
            if SORT_FROM <= s and s + SORT_AHEAD < GROUPS and (s + SORT_AHEAD) % 4 != 0:
                sort_words(s + SORT_AHEAD)
            if 0 <= s - LAG_MX < GROUPS:
                passes(s - LAG_MX)
            if 0 <= s - LAG_ADD < GROUPS:
                adds(s - LAG_ADD)
            if 0 <= s - LAG_TANH < GROUPS:
                finish(s - LAG_TANH)
            if s < GROUPS:
                copies(s)
            if s - 1 < GROUPS:
                quantise(s - 1)
